import numpy as np
import ml_dtypes


def mxq(x, axis, fmt="e4m3"):
    dtype, down = {"e4m3": (ml_dtypes.float8_e4m3fn, 7), "e5m2": (ml_dtypes.float8_e5m2, 14)}[fmt]
    v = np.moveaxis(np.asarray(x, np.float32).astype(ml_dtypes.bfloat16).astype(np.float64), axis, -1)
    blocks = v.reshape(v.shape[:-1] + (-1, 32))
    amax = np.abs(blocks).max(-1, keepdims=True)
    byte = np.maximum(np.where(amax > 0, np.frexp(amax)[1] - 1 + 127, 0) - down, 1)
    scale = np.exp2(byte - 127.0)
    codes = (blocks / scale).astype(np.float32).astype(dtype).astype(np.float64)
    return np.moveaxis((codes * scale).reshape(v.shape), -1, axis)


WIDE = False


def mx_kscale(k):
    if not WIDE:
        return np.ones(k)
    levels = np.array([10, -10, 5, -5, 0])
    if k % 512:
        return np.exp2(np.random.permutation(np.resize(levels, k // 32))).repeat(32)
    a = np.empty((k // 512, 16))
    for p in range(k // 512):
        a[p, :8] = np.random.permutation(np.resize(levels, 8))
        for g in range(8):
            far = levels[np.abs(levels - a[p, g]) >= 10]
            a[p, g + 8] = far[np.random.randint(len(far))]
    return np.exp2(a.ravel()).repeat(32)


BF16 = ml_dtypes.bfloat16


def bf(x):
    return np.asarray(x, np.float32).astype(BF16)


def f64(x):
    return np.asarray(x).astype(np.float64)


B, D, E = 2, 1024, 256
S = E // 2


def rope(y):
    n = y.shape[-1]
    inv_freq = 1.0 / (10000.0 ** (np.arange(0.0, n, 2.0) / n))
    freqs = inv_freq * np.arange(y.shape[1], dtype=np.float64)
    sin = np.sin(freqs)[None, :, None]
    cos = np.cos(freqs)[None, :, None]
    y1 = y[..., ::2]
    y2 = y[..., 1::2]
    return np.concatenate([y1 * cos - y2 * sin, y1 * sin + y2 * cos], axis=-1)


def setup_inputs():
    s = mx_kscale(D)
    return {"x": bf(np.random.standard_normal((B, S, D)) * s),
            "Wk": bf(np.random.standard_normal((E, D)) / np.sqrt(D) / s[None, :]),
            "bk": bf(np.random.standard_normal(E) * 0.3),
            "Wq": bf(np.random.standard_normal((E, D)) / np.sqrt(D) / s[None, :]),
            "bq": bf(np.random.standard_normal(E) * 0.3),
            "Wv": bf(np.random.standard_normal((E, D)) / np.sqrt(D) / s[None, :]),
            "bv": bf(np.random.standard_normal(E) * 0.3)}


def reference(x, Wk, bk, Wq, bq, Wv, bv):
    xq = mxq(f64(x), 2, "e4m3")
    K = rope((xq @ mxq(f64(Wk), 1, "e4m3").T) + f64(bk))
    Q = rope((xq @ mxq(f64(Wq), 1, "e4m3").T) + f64(bq))
    V = (xq @ mxq(f64(Wv), 1, "e4m3").T) + f64(bv)
    return (K, Q, V)

@@ -1,0 +1,213 @@
+from contextlib import ExitStack
+
+import concourse.mybir as mybir
+from concourse.masks import make_identity
+
+F32 = mybir.dt.float32
+BF16 = mybir.dt.bfloat16
+U32 = mybir.dt.uint32
+U8 = mybir.dt.uint8
+FP8X4 = mybir.dt.float8_e4m3fn_x4
+ALU = mybir.AluOpType
+ACT = mybir.ActivationFunctionType
+
+P = 128
+B = 2
+D = 1024
+E = 256
+HALF = E // 2
+PASSES = D // (4 * P)
+WORDS = D // 2
+
+X_TILES = (0, 1)
+K_TILES = (2, 3)
+Q_TILES = (4, 5)
+V_TILES = (6, 7)
+
+FLOPS = 2 * B * P * D * 3 * E
+
+
+def tile_attention_s_kernel(tc, x, Wk, bk, Wq, bq, Wv, bv, out_0, out_1, out_2):
+    nc = tc.nc
+    with ExitStack() as ctx:
+        consts = ctx.enter_context(tc.tile_pool(name="consts", bufs=1))
+        loads = ctx.enter_context(tc.tile_pool(name="loads", bufs=1))
+        stage = ctx.enter_context(tc.tile_pool(name="stage", bufs=3))
+        results = ctx.enter_context(tc.tile_pool(name="results", bufs=1))
+        psum_work = ctx.enter_context(tc.psum_pool(name="psum_work", bufs=5))
+        psum_acc = ctx.enter_context(tc.psum_pool(name="psum_acc", bufs=3))
+
+        bias_rows = consts.tile([P, 3 * E], BF16)
+        nc.vector.memset(bias_rows[:], 0.0)
+        even_odd = "(j e) d -> e j d"
+        sources = [
+            x[0],
+            x[1],
+            Wk.rearrange(even_odd, e=2)[0],
+            Wk.rearrange(even_odd, e=2)[1],
+            Wq.rearrange(even_odd, e=2)[0],
+            Wq.rearrange(even_odd, e=2)[1],
+            Wv[0:HALF, :],
+            Wv[HALF:E, :],
+        ]
+        raw = []
+        for i, source in enumerate(sources):
+            raw_i = loads.tile([P, D], BF16, name="raw%d" % i)
+            nc.sync.dma_start(out=raw_i[:], in_=source)
+            raw.append(raw_i)
+            if i == X_TILES[-1]:
+                for w, bias in enumerate((bk, bq, bv)):
+                    nc.sync.dma_start(
+                        out=bias_rows[0:1, w * E : (w + 1) * E],
+                        in_=bias.rearrange("(o e) -> o e", o=1),
+                    )
+
+        ident = consts.tile([P, P], F32)
+        make_identity(nc, ident[:])
+        ones = consts.tile([P, P], BF16)
+        nc.vector.memset(ones[:], 1.0)
+
+        pos = consts.tile([P, 1], F32)
+        nc.gpsimd.iota(
+            pos[:], pattern=[[0, 1]], base=0, channel_multiplier=1,
+            allow_small_or_imprecise_dtypes=True,
+        )
+        exponent = consts.tile([P, 1], F32)
+        nc.gpsimd.tensor_scalar(
+            out=exponent[:], in0=pos[:], scalar1=-2.0 / E, scalar2=0.0, op0=ALU.mult, op1=ALU.add
+        )
+        ten_thousand = consts.tile([P, 1], F32)
+        nc.gpsimd.memset(ten_thousand[:], 10000.0)
+        theta = consts.tile([P, 1], F32)
+        nc.gpsimd.tensor_tensor(out=theta[:], in0=ten_thousand[:], in1=exponent[:], op=ALU.pow)
+        nc.gpsimd.tensor_tensor(out=theta[:], in0=theta[:], in1=pos[:], op=ALU.mult)
+        sines = consts.tile([P, 2], F32)
+        nc.scalar.activation(out=sines[:, 0:1], in_=theta[:], func=ACT.Sin, scale=0.5)
+        nc.scalar.activation(out=sines[:, 1:2], in_=theta[:], func=ACT.Sin, scale=0.25)
+
+        codes = consts.tile([P, len(sources), PASSES, P], U32, align_bytes=64)
+        scales = consts.tile([P, len(sources), PASSES, P], U8, align_bytes=64)
+
+        def transpose(i, copy_out):
+            words = raw[i][:].bitcast(F32)
+            turned = psum_work.tile([P, WORDS // P, P], F32, tag="work")
+            for c in range(WORDS // P):
+                nc.tensor.transpose(turned[:, c, :], words[:, 2 * P * (c // 2) + c % 2 : 2 * P * (c // 2 + 1) : 2], ident[:])
+            grouped = stage.tile([P, D], BF16, align_bytes=64)
+            copy_out(
+                out=grouped[:].bitcast(F32).rearrange("q (g r u) -> q g r u", g=PASSES, u=2),
+                in_=turned[:].rearrange("q (g u) r -> q g r u", u=2),
+            )
+            return grouped
+
+        def quantise(i, grouped):
+            nc.vector.quantize_mx(
+                out=codes[:, i].rearrange("q g r -> q (g r)").bitcast(FP8X4),
+                scales=scales[:, i].rearrange("q g r -> q (g r)"),
+                in_=grouped[:],
+            )
+
+        def project(acc_columns, i):
+            for b in X_TILES:
+                for g in range(PASSES):
+                    nc.tensor.matmul_mx(
+                        out=acc_columns[:, b, :],
+                        lhsT=codes[:, b, g, :].bitcast(FP8X4),
+                        lhsT_scale=scales[:, b, g, :],
+                        rhs=codes[:, i, g, :].bitcast(FP8X4),
+                        rhs_scale=scales[:, i, g, :],
+                        start=(g == 0),
+                        stop=(g == PASSES - 1),
+                    )
+
+        def project_rotate_store(tiles, bias_rot_w, out_w):
+            acc = psum_acc.tile([P, B, 2, HALF], F32, tag="acc")
+            for half, i in enumerate(tiles):
+                project(acc[:, :, half, :], i)
+            rotated = results.tile([P, B, 2, HALF], F32, name="rotated%d" % tiles[0])
+            nc.vector.scalar_tensor_tensor(
+                out=rotated[:].rearrange("p b h j -> p b (h j)"),
+                in0=acc[:].rearrange("p b h j -> p b (h j)"),
+                scalar=cos,
+                in1=bias_rot_w.rearrange("p h j -> p (h j)").unsqueeze(1).to_broadcast([P, B, E]),
+                op0=ALU.mult, op1=ALU.add,
+            )
+            nc.vector.scalar_tensor_tensor(
+                out=rotated[:, :, 0, :], in0=acc[:, :, 1, :], scalar=neg_sin,
+                in1=rotated[:, :, 0, :], op0=ALU.mult, op1=ALU.add,
+            )
+            nc.vector.scalar_tensor_tensor(
+                out=rotated[:, :, 1, :], in0=acc[:, :, 0, :], scalar=sin,
+                in1=rotated[:, :, 1, :], op0=ALU.mult, op1=ALU.add,
+            )
+            nc.sync.dma_start(
+                out=out_w.rearrange("b s e -> s b e"),
+                in_=rotated[:].rearrange("p b h j -> p b (h j)"),
+            )
+
+        grouped_x = [transpose(i, nc.scalar.copy) for i in X_TILES]
+        for i in X_TILES:
+            quantise(i, grouped_x[i])
+
+        cosines = consts.tile([P, 2], F32)
+        nc.vector.scalar_tensor_tensor(
+            out=cosines[:], in0=sines[:], scalar=-2.0, in1=sines[:], op0=ALU.mult, op1=ALU.mult
+        )
+        nc.vector.tensor_scalar_add(out=cosines[:], in0=cosines[:], scalar1=1.0)
+        cos = cosines[:, 0:1]
+        plus_minus_sin = consts.tile([P, 2], F32)
+        for column, factor in enumerate((2.0, -2.0)):
+            nc.vector.scalar_tensor_tensor(
+                out=plus_minus_sin[:, column : column + 1],
+                in0=sines[:, 0:1], scalar=factor, in1=cosines[:, 1:2],
+                op0=ALU.mult, op1=ALU.mult,
+            )
+        sin = plus_minus_sin[:, 0:1]
+        neg_sin = plus_minus_sin[:, 1:2]
+
+        for i in K_TILES:
+            quantise(i, transpose(i, nc.scalar.copy))
+
+        bias_kq = psum_work.tile([P, 2, HALF, 2], F32, tag="work")
+        nc.tensor.matmul(
+            out=bias_kq[:].rearrange("p w j e -> p (w j e)"),
+            lhsT=ones[:], rhs=bias_rows[:, 0 : 2 * E], start=True, stop=True,
+        )
+        bias_v_bank = psum_work.tile([P, E], F32, tag="work")
+        nc.tensor.matmul(
+            out=bias_v_bank[:], lhsT=ones[:], rhs=bias_rows[:, 2 * E : 3 * E], start=True, stop=True
+        )
+        bias_rot = consts.tile([P, 2, 2, HALF], F32)
+        bias_even = bias_kq[:, :, :, 0]
+        bias_odd = bias_kq[:, :, :, 1]
+        nc.scalar.activation(out=bias_rot[:, :, 0, :], in_=bias_odd, func=ACT.Copy, scale=neg_sin)
+        nc.scalar.activation(out=bias_rot[:, :, 1, :], in_=bias_even, func=ACT.Copy, scale=sin)
+        nc.vector.scalar_tensor_tensor(
+            out=bias_rot[:, :, 0, :], in0=bias_even, scalar=cos, in1=bias_rot[:, :, 0, :],
+            op0=ALU.mult, op1=ALU.add,
+        )
+        nc.vector.scalar_tensor_tensor(
+            out=bias_rot[:, :, 1, :], in0=bias_odd, scalar=cos, in1=bias_rot[:, :, 1, :],
+            op0=ALU.mult, op1=ALU.add,
+        )
+
+        for i in Q_TILES:
+            quantise(i, transpose(i, nc.scalar.copy))
+        project_rotate_store(K_TILES, bias_rot[:, 0], out_0)
+
+        bias_v = consts.tile([P, E], F32)
+        nc.scalar.copy(out=bias_v[:], in_=bias_v_bank[:])
+        for i in V_TILES:
+            quantise(i, transpose(i, nc.scalar.copy))
+        project_rotate_store(Q_TILES, bias_rot[:, 1], out_1)
+
+        for half, i in enumerate(V_TILES):
+            columns = slice(half * HALF, (half + 1) * HALF)
+            acc_v = psum_acc.tile([P, B, HALF], F32, tag="acc")
+            project(acc_v, i)
+            v_half = results.tile([P, B, HALF], F32, name="v_half%d" % half)
+            nc.vector.tensor_tensor(
+                out=v_half[:], in0=acc_v[:],
+                in1=bias_v[:, columns].unsqueeze(1).to_broadcast([P, B, HALF]), op=ALU.add,
+            )
+            nc.sync.dma_start(out=out_2.rearrange("b s e -> s b e")[:, :, columns], in_=v_half[:])

@@ -19,6 +19,8 @@ HALF = E // 2
 PASSES = D // (4 * P)
 WORDS = D // 2
 
+WARM_COLUMNS = 256
+
 X_TILES = (0, 1)
 K_TILES = (2, 3)
 Q_TILES = (4, 5)
@@ -37,8 +39,6 @@ def tile_attention_s_kernel(tc, x, Wk, bk, Wq, bq, Wv, bv, out_0, out_1, out_2):
         psum_work = ctx.enter_context(tc.psum_pool(name="psum_work", bufs=5))
         psum_acc = ctx.enter_context(tc.psum_pool(name="psum_acc", bufs=3))
 
-        bias_rows = consts.tile([P, 3 * E], BF16)
-        nc.vector.memset(bias_rows[:], 0.0)
         even_odd = "(j e) d -> e j d"
         sources = [
             x[0],
@@ -50,22 +50,28 @@ def tile_attention_s_kernel(tc, x, Wk, bk, Wq, bq, Wv, bv, out_0, out_1, out_2):
             Wv[0:HALF, :],
             Wv[HALF:E, :],
         ]
+        bias_all = consts.tile([P, 3, E], BF16)
         raw = []
         for i, source in enumerate(sources):
             raw_i = loads.tile([P, D], BF16, name="raw%d" % i)
-            nc.sync.dma_start(out=raw_i[:], in_=source)
+            if i == 0:
+                for g in range(PASSES):
+                    half = slice(g * (D // 2), (g + 1) * (D // 2))
+                    nc.sync.dma_start(out=raw_i[:, half], in_=source[:, half])
+            else:
+                nc.sync.dma_start(out=raw_i[:], in_=source)
             raw.append(raw_i)
-            if i == X_TILES[-1]:
+            if i == K_TILES[-1]:
                 for w, bias in enumerate((bk, bq, bv)):
-                    nc.sync.dma_start(
-                        out=bias_rows[0:1, w * E : (w + 1) * E],
-                        in_=bias.rearrange("(o e) -> o e", o=1),
-                    )
+                    nc.sync.dma_start(out=bias_all[:, w, :], in_=bias.partition_broadcast(P))
+
+        zeros = consts.tile([P, WARM_COLUMNS], F32)
+        nc.vector.memset(zeros[:], 0.0)
+        warm = psum_work.tile([P, WARM_COLUMNS], F32, tag="work", name="warm")
+        nc.tensor.matmul(out=warm[:], lhsT=zeros[:, 0:P], rhs=zeros[:], start=True, stop=True)
 
         ident = consts.tile([P, P], F32)
         make_identity(nc, ident[:])
-        ones = consts.tile([P, P], BF16)
-        nc.vector.memset(ones[:], 1.0)
 
         pos = consts.tile([P, 1], F32)
         nc.gpsimd.iota(
@@ -85,70 +91,6 @@ def tile_attention_s_kernel(tc, x, Wk, bk, Wq, bq, Wv, bv, out_0, out_1, out_2):
         nc.scalar.activation(out=sines[:, 0:1], in_=theta[:], func=ACT.Sin, scale=0.5)
         nc.scalar.activation(out=sines[:, 1:2], in_=theta[:], func=ACT.Sin, scale=0.25)
 
-        codes = consts.tile([P, len(sources), PASSES, P], U32, align_bytes=64)
-        scales = consts.tile([P, len(sources), PASSES, P], U8, align_bytes=64)
-
-        def transpose(i, copy_out):
-            words = raw[i][:].bitcast(F32)
-            turned = psum_work.tile([P, WORDS // P, P], F32, tag="work")
-            for c in range(WORDS // P):
-                nc.tensor.transpose(turned[:, c, :], words[:, 2 * P * (c // 2) + c % 2 : 2 * P * (c // 2 + 1) : 2], ident[:])
-            grouped = stage.tile([P, D], BF16, align_bytes=64)
-            copy_out(
-                out=grouped[:].bitcast(F32).rearrange("q (g r u) -> q g r u", g=PASSES, u=2),
-                in_=turned[:].rearrange("q (g u) r -> q g r u", u=2),
-            )
-            return grouped
-
-        def quantise(i, grouped):
-            nc.vector.quantize_mx(
-                out=codes[:, i].rearrange("q g r -> q (g r)").bitcast(FP8X4),
-                scales=scales[:, i].rearrange("q g r -> q (g r)"),
-                in_=grouped[:],
-            )
-
-        def project(acc_columns, i):
-            for b in X_TILES:
-                for g in range(PASSES):
-                    nc.tensor.matmul_mx(
-                        out=acc_columns[:, b, :],
-                        lhsT=codes[:, b, g, :].bitcast(FP8X4),
-                        lhsT_scale=scales[:, b, g, :],
-                        rhs=codes[:, i, g, :].bitcast(FP8X4),
-                        rhs_scale=scales[:, i, g, :],
-                        start=(g == 0),
-                        stop=(g == PASSES - 1),
-                    )
-
-        def project_rotate_store(tiles, bias_rot_w, out_w):
-            acc = psum_acc.tile([P, B, 2, HALF], F32, tag="acc")
-            for half, i in enumerate(tiles):
-                project(acc[:, :, half, :], i)
-            rotated = results.tile([P, B, 2, HALF], F32, name="rotated%d" % tiles[0])
-            nc.vector.scalar_tensor_tensor(
-                out=rotated[:].rearrange("p b h j -> p b (h j)"),
-                in0=acc[:].rearrange("p b h j -> p b (h j)"),
-                scalar=cos,
-                in1=bias_rot_w.rearrange("p h j -> p (h j)").unsqueeze(1).to_broadcast([P, B, E]),
-                op0=ALU.mult, op1=ALU.add,
-            )
-            nc.vector.scalar_tensor_tensor(
-                out=rotated[:, :, 0, :], in0=acc[:, :, 1, :], scalar=neg_sin,
-                in1=rotated[:, :, 0, :], op0=ALU.mult, op1=ALU.add,
-            )
-            nc.vector.scalar_tensor_tensor(
-                out=rotated[:, :, 1, :], in0=acc[:, :, 0, :], scalar=sin,
-                in1=rotated[:, :, 1, :], op0=ALU.mult, op1=ALU.add,
-            )
-            nc.sync.dma_start(
-                out=out_w.rearrange("b s e -> s b e"),
-                in_=rotated[:].rearrange("p b h j -> p b (h j)"),
-            )
-
-        grouped_x = [transpose(i, nc.scalar.copy) for i in X_TILES]
-        for i in X_TILES:
-            quantise(i, grouped_x[i])
-
         cosines = consts.tile([P, 2], F32)
         nc.vector.scalar_tensor_tensor(
             out=cosines[:], in0=sines[:], scalar=-2.0, in1=sines[:], op0=ALU.mult, op1=ALU.mult
@@ -165,49 +107,149 @@ def tile_attention_s_kernel(tc, x, Wk, bk, Wq, bq, Wv, bv, out_0, out_1, out_2):
         sin = plus_minus_sin[:, 0:1]
         neg_sin = plus_minus_sin[:, 1:2]
 
-        for i in K_TILES:
-            quantise(i, transpose(i, nc.scalar.copy))
+        codes = consts.tile([P, len(sources), PASSES, P], U32, align_bytes=64)
+        scales = consts.tile([P, len(sources), PASSES, P], U8, align_bytes=64)
 
-        bias_kq = psum_work.tile([P, 2, HALF, 2], F32, tag="work")
-        nc.tensor.matmul(
-            out=bias_kq[:].rearrange("p w j e -> p (w j e)"),
-            lhsT=ones[:], rhs=bias_rows[:, 0 : 2 * E], start=True, stop=True,
-        )
-        bias_v_bank = psum_work.tile([P, E], F32, tag="work")
-        nc.tensor.matmul(
-            out=bias_v_bank[:], lhsT=ones[:], rhs=bias_rows[:, 2 * E : 3 * E], start=True, stop=True
-        )
+        def transpose(i, passes=range(PASSES)):
+            words = raw[i][:].bitcast(F32)
+            turned = psum_work.tile([P, len(passes), 2, P], F32, tag="work", name="turned")
+            for n, g in enumerate(passes):
+                for u in (0, 1):
+                    first = 2 * P * g + u
+                    nc.tensor.transpose(
+                        turned[:, n, u, :], words[:, first : 2 * P * (g + 1) : 2], ident[:]
+                    )
+            return turned
+
+        def copy_out(turned, passes=range(PASSES)):
+            grouped = stage.tile([P, len(passes) * 4 * P], BF16, align_bytes=64, tag="grouped", name="grouped")
+            nc.scalar.copy(
+                out=grouped[:].bitcast(F32).rearrange("q (g r u) -> q g r u", g=len(passes), u=2),
+                in_=turned[:].rearrange("q g u r -> q g r u"),
+            )
+            return grouped
+
+        def quantise(i, grouped, passes=range(PASSES)):
+            window = slice(passes[0], passes[-1] + 1)
+            nc.vector.quantize_mx(
+                out=codes[:, i, window].rearrange("q g r -> q (g r)").bitcast(FP8X4),
+                scales=scales[:, i, window].rearrange("q g r -> q (g r)"),
+                in_=grouped[:],
+            )
+
+        def project(acc_columns, i):
+            for b in X_TILES:
+                for g in range(PASSES):
+                    nc.tensor.matmul_mx(
+                        out=acc_columns[:, b, :],
+                        lhsT=codes[:, b, g, :].bitcast(FP8X4),
+                        lhsT_scale=scales[:, b, g, :],
+                        rhs=codes[:, i, g, :].bitcast(FP8X4),
+                        rhs_scale=scales[:, i, g, :],
+                        start=(g == 0),
+                        stop=(g == PASSES - 1),
+                    )
+
+        def project_pair(tiles):
+            acc = psum_acc.tile([P, B, 2, HALF], F32, tag="acc", name="acc")
+            for half, i in enumerate(tiles):
+                project(acc[:, :, half, :], i)
+            return acc
+
         bias_rot = consts.tile([P, 2, 2, HALF], F32)
-        bias_even = bias_kq[:, :, :, 0]
-        bias_odd = bias_kq[:, :, :, 1]
-        nc.scalar.activation(out=bias_rot[:, :, 0, :], in_=bias_odd, func=ACT.Copy, scale=neg_sin)
-        nc.scalar.activation(out=bias_rot[:, :, 1, :], in_=bias_even, func=ACT.Copy, scale=sin)
-        nc.vector.scalar_tensor_tensor(
-            out=bias_rot[:, :, 0, :], in0=bias_even, scalar=cos, in1=bias_rot[:, :, 0, :],
-            op0=ALU.mult, op1=ALU.add,
-        )
-        nc.vector.scalar_tensor_tensor(
-            out=bias_rot[:, :, 1, :], in0=bias_odd, scalar=cos, in1=bias_rot[:, :, 1, :],
-            op0=ALU.mult, op1=ALU.add,
-        )
 
-        for i in Q_TILES:
-            quantise(i, transpose(i, nc.scalar.copy))
-        project_rotate_store(K_TILES, bias_rot[:, 0], out_0)
+        def rotate_cos(w, acc):
+            rotated = results.tile([P, B, 2, HALF], F32, name="rotated%d" % w)
+            nc.vector.scalar_tensor_tensor(
+                out=rotated[:].rearrange("p b h j -> p b (h j)"),
+                in0=acc[:].rearrange("p b h j -> p b (h j)"),
+                scalar=cos,
+                in1=bias_rot[:, w].rearrange("p h j -> p (h j)").unsqueeze(1).to_broadcast([P, B, E]),
+                op0=ALU.mult, op1=ALU.add,
+            )
+            return rotated
 
-        bias_v = consts.tile([P, E], F32)
-        nc.scalar.copy(out=bias_v[:], in_=bias_v_bank[:])
-        for i in V_TILES:
-            quantise(i, transpose(i, nc.scalar.copy))
-        project_rotate_store(Q_TILES, bias_rot[:, 1], out_1)
+        def rotate_sin(acc, rotated, half):
+            nc.vector.scalar_tensor_tensor(
+                out=rotated[:, :, half, :], in0=acc[:, :, 1 - half, :],
+                scalar=(neg_sin, sin)[half], in1=rotated[:, :, half, :],
+                op0=ALU.mult, op1=ALU.add,
+            )
 
-        for half, i in enumerate(V_TILES):
+        def store(rotated, out_w):
+            nc.sync.dma_start(
+                out=out_w.rearrange("b s e -> s b e"),
+                in_=rotated[:].rearrange("p b h j -> p b (h j)"),
+            )
+
+        def add_store_v(half, acc_v):
             columns = slice(half * HALF, (half + 1) * HALF)
-            acc_v = psum_acc.tile([P, B, HALF], F32, tag="acc")
-            project(acc_v, i)
             v_half = results.tile([P, B, HALF], F32, name="v_half%d" % half)
             nc.vector.tensor_tensor(
                 out=v_half[:], in0=acc_v[:],
-                in1=bias_v[:, columns].unsqueeze(1).to_broadcast([P, B, HALF]), op=ALU.add,
+                in1=bias_all[:, 2, columns].unsqueeze(1).to_broadcast([P, B, HALF]), op=ALU.add,
             )
             nc.sync.dma_start(out=out_2.rearrange("b s e -> s b e")[:, :, columns], in_=v_half[:])
+
+        bias_kq = bias_all[:, 0:2, :].rearrange("p w (j e) -> p w j e", e=2)
+
+        def rotate_bias_sin(half):
+            nc.vector.tensor_scalar(
+                out=bias_rot[:, :, half, :], in0=bias_kq[:, :, :, 1 - half],
+                scalar1=(neg_sin, sin)[half], scalar2=None, op0=ALU.mult,
+            )
+
+        def rotate_bias_cos(half):
+            nc.vector.scalar_tensor_tensor(
+                out=bias_rot[:, :, half, :], in0=bias_kq[:, :, :, half], scalar=cos,
+                in1=bias_rot[:, :, half, :], op0=ALU.mult, op1=ALU.add,
+            )
+
+        with tc.manual_schedule():
+            g_parts = [range(g, g + 1) for g in range(PASSES)]
+            turned_x0 = [transpose(0, part) for part in g_parts]
+            grouped_x0 = [copy_out(t, part) for t, part in zip(turned_x0, g_parts)]
+            turned = transpose(1)
+            for part, grouped_half in zip(g_parts, grouped_x0):
+                quantise(0, grouped_half, part)
+            grouped = copy_out(turned)
+            turned = transpose(2)
+            quantise(1, grouped)
+            rotate_bias_sin(0)
+            grouped = copy_out(turned)
+            turned = transpose(3)
+            quantise(2, grouped)
+            rotate_bias_sin(1)
+            grouped = copy_out(turned)
+            turned = transpose(4)
+            quantise(3, grouped)
+            rotate_bias_cos(0)
+            grouped = copy_out(turned)
+            turned = transpose(5)
+            quantise(4, grouped)
+            rotate_bias_cos(1)
+            grouped = copy_out(turned)
+            acc_k = project_pair(K_TILES)
+            turned = transpose(6)
+            quantise(5, grouped)
+            rotated_k = rotate_cos(0, acc_k)
+            grouped = copy_out(turned)
+            acc_q = project_pair(Q_TILES)
+            turned_v1 = [transpose(7, part) for part in g_parts]
+            rotate_sin(acc_k, rotated_k, 0)
+            rotate_sin(acc_k, rotated_k, 1)
+            store(rotated_k, out_0)
+            quantise(6, grouped)
+            grouped_v1 = [copy_out(t, part) for t, part in zip(turned_v1, g_parts)]
+            acc_v0 = psum_acc.tile([P, B, HALF], F32, tag="acc", name="acc_v0")
+            project(acc_v0, 6)
+            rotated_q = rotate_cos(1, acc_q)
+            quantise(7, grouped_v1[0], g_parts[0])
+            quantise(7, grouped_v1[1], g_parts[1])
+            acc_v1 = psum_acc.tile([P, B, HALF], F32, tag="acc", name="acc_v1")
+            project(acc_v1, 7)
+            rotate_sin(acc_q, rotated_q, 0)
+            rotate_sin(acc_q, rotated_q, 1)
+            store(rotated_q, out_1)
+            add_store_v(0, acc_v0)
+            add_store_v(1, acc_v1)

@@ -50,7 +50,7 @@ def tile_attention_s_kernel(tc, x, Wk, bk, Wq, bq, Wv, bv, out_0, out_1, out_2):
             Wv[0:HALF, :],
             Wv[HALF:E, :],
         ]
-        bias_all = consts.tile([P, 3, E], BF16)
+        bias_words = []
         raw = []
         for i, source in enumerate(sources):
             raw_i = loads.tile([P, D], BF16, name="raw%d" % i)
@@ -61,9 +61,11 @@ def tile_attention_s_kernel(tc, x, Wk, bk, Wq, bq, Wv, bv, out_0, out_1, out_2):
             else:
                 nc.sync.dma_start(out=raw_i[:], in_=source)
             raw.append(raw_i)
-            if i == K_TILES[-1]:
+            if i == X_TILES[-1]:
                 for w, bias in enumerate((bk, bq, bv)):
-                    nc.sync.dma_start(out=bias_all[:, w, :], in_=bias.partition_broadcast(P))
+                    words_w = consts.tile([P, 2], BF16, name="bias_words%d" % w)
+                    nc.sync.dma_start(out=words_w[:], in_=bias.rearrange("(p e) -> p e", e=2))
+                    bias_words.append(words_w)
 
         zeros = consts.tile([P, WARM_COLUMNS], F32)
         nc.vector.memset(zeros[:], 0.0)
@@ -187,11 +189,20 @@ def tile_attention_s_kernel(tc, x, Wk, bk, Wq, bq, Wv, bv, out_0, out_1, out_2):
             v_half = results.tile([P, B, HALF], F32, name="v_half%d" % half)
             nc.vector.tensor_tensor(
                 out=v_half[:], in0=acc_v[:],
-                in1=bias_all[:, 2, columns].unsqueeze(1).to_broadcast([P, B, HALF]), op=ALU.add,
+                in1=bias_v[:, columns].unsqueeze(1).to_broadcast([P, B, HALF]), op=ALU.add,
             )
             nc.sync.dma_start(out=out_2.rearrange("b s e -> s b e")[:, :, columns], in_=v_half[:])
 
+        bias_bank = psum_acc.tile([P, 3, P], F32, tag="acc", name="bias_bank")
+        bias_all = bias_bank[:].bitcast(BF16)
         bias_kq = bias_all[:, 0:2, :].rearrange("p w (j e) -> p w j e", e=2)
+        bias_v = consts.tile([P, E], F32)
+
+        def spread_biases():
+            for w in range(3):
+                nc.tensor.transpose(
+                    bias_bank[:, w, :], bias_words[w][:].bitcast(F32).to_broadcast([P, P]), ident[:]
+                )
 
         def rotate_bias_sin(half):
             nc.vector.tensor_scalar(
@@ -215,9 +226,10 @@ def tile_attention_s_kernel(tc, x, Wk, bk, Wq, bq, Wv, bv, out_0, out_1, out_2):
             grouped = copy_out(turned)
             turned = transpose(2)
             quantise(1, grouped)
-            rotate_bias_sin(0)
             grouped = copy_out(turned)
+            spread_biases()
             turned = transpose(3)
+            rotate_bias_sin(0)
             quantise(2, grouped)
             rotate_bias_sin(1)
             grouped = copy_out(turned)
@@ -231,6 +243,7 @@ def tile_attention_s_kernel(tc, x, Wk, bk, Wq, bq, Wv, bv, out_0, out_1, out_2):
             grouped = copy_out(turned)
             acc_k = project_pair(K_TILES)
             turned = transpose(6)
+            nc.scalar.copy(out=bias_v[:], in_=bias_all[:, 2, :])
             quantise(5, grouped)
             rotated_k = rotate_cos(0, acc_k)
             grouped = copy_out(turned)

@@ -50,7 +50,12 @@ def tile_attention_s_kernel(tc, x, Wk, bk, Wq, bq, Wv, bv, out_0, out_1, out_2):
             Wv[0:HALF, :],
             Wv[HALF:E, :],
         ]
-        bias_words = []
+        bias_rows = consts.tile([P, 3 * E], BF16)
+        zeros = consts.tile([P, WARM_COLUMNS], F32)
+        nc.vector.memset(zeros[:], 0.0)
+        nc.vector.memset(bias_rows[:], 0.0)
+        ones = consts.tile([P, P], BF16)
+        nc.vector.memset(ones[:], 1.0)
         raw = []
         for i, source in enumerate(sources):
             raw_i = loads.tile([P, D], BF16, name="raw%d" % i)
@@ -63,12 +68,11 @@ def tile_attention_s_kernel(tc, x, Wk, bk, Wq, bq, Wv, bv, out_0, out_1, out_2):
             raw.append(raw_i)
             if i == X_TILES[-1]:
                 for w, bias in enumerate((bk, bq, bv)):
-                    words_w = consts.tile([P, 2], BF16, name="bias_words%d" % w)
-                    nc.sync.dma_start(out=words_w[:], in_=bias.rearrange("(p e) -> p e", e=2))
-                    bias_words.append(words_w)
+                    nc.sync.dma_start(
+                        out=bias_rows[0:1, w * E : (w + 1) * E],
+                        in_=bias.rearrange("(o e) -> o e", o=1),
+                    )
 
-        zeros = consts.tile([P, WARM_COLUMNS], F32)
-        nc.vector.memset(zeros[:], 0.0)
         warm = psum_work.tile([P, WARM_COLUMNS], F32, tag="work", name="warm")
         nc.tensor.matmul(out=warm[:], lhsT=zeros[:, 0:P], rhs=zeros[:], start=True, stop=True)
 
@@ -193,16 +197,19 @@ def tile_attention_s_kernel(tc, x, Wk, bk, Wq, bq, Wv, bv, out_0, out_1, out_2):
             )
             nc.sync.dma_start(out=out_2.rearrange("b s e -> s b e")[:, :, columns], in_=v_half[:])
 
-        bias_bank = psum_acc.tile([P, 3, P], F32, tag="acc", name="bias_bank")
-        bias_all = bias_bank[:].bitcast(BF16)
-        bias_kq = bias_all[:, 0:2, :].rearrange("p w (j e) -> p w j e", e=2)
+        bias_kq_bank = psum_acc.tile([P, 2 * E], F32, tag="acc", name="bias_kq_bank")
+        bias_v_bank = psum_work.tile([P, E], F32, tag="work", name="bias_v_bank")
+        bias_kq = bias_kq_bank[:].rearrange("p (w j e) -> p w j e", w=2, e=2)
         bias_v = consts.tile([P, E], F32)
 
         def spread_biases():
-            for w in range(3):
-                nc.tensor.transpose(
-                    bias_bank[:, w, :], bias_words[w][:].bitcast(F32).to_broadcast([P, P]), ident[:]
-                )
+            nc.tensor.matmul(
+                out=bias_kq_bank[:], lhsT=ones[:], rhs=bias_rows[:, 0 : 2 * E], start=True, stop=True
+            )
+            nc.tensor.matmul(
+                out=bias_v_bank[:], lhsT=ones[:], rhs=bias_rows[:, 2 * E : 3 * E],
+                start=True, stop=True,
+            )
 
         def rotate_bias_sin(half):
             nc.vector.tensor_scalar(
@@ -229,6 +236,7 @@ def tile_attention_s_kernel(tc, x, Wk, bk, Wq, bq, Wv, bv, out_0, out_1, out_2):
             grouped = copy_out(turned)
             spread_biases()
             turned = transpose(3)
+            nc.scalar.copy(out=bias_v[:], in_=bias_v_bank[:])
             rotate_bias_sin(0)
             quantise(2, grouped)
             rotate_bias_sin(1)
@@ -243,7 +251,6 @@ def tile_attention_s_kernel(tc, x, Wk, bk, Wq, bq, Wv, bv, out_0, out_1, out_2):
             grouped = copy_out(turned)
             acc_k = project_pair(K_TILES)
             turned = transpose(6)
-            nc.scalar.copy(out=bias_v[:], in_=bias_all[:, 2, :])
             quantise(5, grouped)
             rotated_k = rotate_cos(0, acc_k)
             grouped = copy_out(turned)

from contextlib import ExitStack

import concourse.mybir as mybir
from concourse.masks import make_identity

F32 = mybir.dt.float32
BF16 = mybir.dt.bfloat16
U32 = mybir.dt.uint32
U8 = mybir.dt.uint8
FP8X4 = mybir.dt.float8_e4m3fn_x4
ALU = mybir.AluOpType
ACT = mybir.ActivationFunctionType

P = 128
B = 2
D = 1024
E = 256
HALF = E // 2
PASSES = D // (4 * P)
WORDS = D // 2

WARM_COLUMNS = 256

X_TILES = (0, 1)
K_TILES = (2, 3)
Q_TILES = (4, 5)
V_TILES = (6, 7)

FLOPS = 2 * B * P * D * 3 * E


def tile_attention_s_kernel(tc, x, Wk, bk, Wq, bq, Wv, bv, out_0, out_1, out_2):
    nc = tc.nc
    with ExitStack() as ctx:
        consts = ctx.enter_context(tc.tile_pool(name="consts", bufs=1))
        loads = ctx.enter_context(tc.tile_pool(name="loads", bufs=1))
        stage = ctx.enter_context(tc.tile_pool(name="stage", bufs=3))
        results = ctx.enter_context(tc.tile_pool(name="results", bufs=1))
        psum_work = ctx.enter_context(tc.psum_pool(name="psum_work", bufs=5))
        psum_acc = ctx.enter_context(tc.psum_pool(name="psum_acc", bufs=3))

        even_odd = "(j e) d -> e j d"
        sources = [
            x[0],
            x[1],
            Wk.rearrange(even_odd, e=2)[0],
            Wk.rearrange(even_odd, e=2)[1],
            Wq.rearrange(even_odd, e=2)[0],
            Wq.rearrange(even_odd, e=2)[1],
            Wv[0:HALF, :],
            Wv[HALF:E, :],
        ]
        bias_rows = consts.tile([P, 3 * E], BF16)
        zeros = consts.tile([P, WARM_COLUMNS], F32)
        nc.vector.memset(zeros[:], 0.0)
        nc.vector.memset(bias_rows[:], 0.0)
        ones = consts.tile([P, P], BF16)
        nc.vector.memset(ones[:], 1.0)
        raw = []
        for i, source in enumerate(sources):
            raw_i = loads.tile([P, D], BF16, name="raw%d" % i)
            if i == 0:
                for g in range(PASSES):
                    half = slice(g * (D // 2), (g + 1) * (D // 2))
                    nc.sync.dma_start(out=raw_i[:, half], in_=source[:, half])
            else:
                nc.sync.dma_start(out=raw_i[:], in_=source)
            raw.append(raw_i)
            if i == X_TILES[-1]:
                for w, bias in enumerate((bk, bq, bv)):
                    nc.sync.dma_start(
                        out=bias_rows[0:1, w * E : (w + 1) * E],
                        in_=bias.rearrange("(o e) -> o e", o=1),
                    )

        warm = psum_work.tile([P, WARM_COLUMNS], F32, tag="work", name="warm")
        nc.tensor.matmul(out=warm[:], lhsT=zeros[:, 0:P], rhs=zeros[:], start=True, stop=True)

        ident = consts.tile([P, P], F32)
        make_identity(nc, ident[:])

        pos = consts.tile([P, 1], F32)
        nc.gpsimd.iota(
            pos[:], pattern=[[0, 1]], base=0, channel_multiplier=1,
            allow_small_or_imprecise_dtypes=True,
        )
        exponent = consts.tile([P, 1], F32)
        nc.gpsimd.tensor_scalar(
            out=exponent[:], in0=pos[:], scalar1=-2.0 / E, scalar2=0.0, op0=ALU.mult, op1=ALU.add
        )
        ten_thousand = consts.tile([P, 1], F32)
        nc.gpsimd.memset(ten_thousand[:], 10000.0)
        theta = consts.tile([P, 1], F32)
        nc.gpsimd.tensor_tensor(out=theta[:], in0=ten_thousand[:], in1=exponent[:], op=ALU.pow)
        nc.gpsimd.tensor_tensor(out=theta[:], in0=theta[:], in1=pos[:], op=ALU.mult)
        sines = consts.tile([P, 2], F32)
        nc.scalar.activation(out=sines[:, 0:1], in_=theta[:], func=ACT.Sin, scale=0.5)
        nc.scalar.activation(out=sines[:, 1:2], in_=theta[:], func=ACT.Sin, scale=0.25)

        cosines = consts.tile([P, 2], F32)
        nc.vector.scalar_tensor_tensor(
            out=cosines[:], in0=sines[:], scalar=-2.0, in1=sines[:], op0=ALU.mult, op1=ALU.mult
        )
        nc.vector.tensor_scalar_add(out=cosines[:], in0=cosines[:], scalar1=1.0)
        cos = cosines[:, 0:1]
        plus_minus_sin = consts.tile([P, 2], F32)
        for column, factor in enumerate((2.0, -2.0)):
            nc.vector.scalar_tensor_tensor(
                out=plus_minus_sin[:, column : column + 1],
                in0=sines[:, 0:1], scalar=factor, in1=cosines[:, 1:2],
                op0=ALU.mult, op1=ALU.mult,
            )
        sin = plus_minus_sin[:, 0:1]
        neg_sin = plus_minus_sin[:, 1:2]

        codes = consts.tile([P, len(sources), PASSES, P], U32, align_bytes=64)
        scales = consts.tile([P, len(sources), PASSES, P], U8, align_bytes=64)

        def transpose(i, passes=range(PASSES)):
            words = raw[i][:].bitcast(F32)
            turned = psum_work.tile([P, len(passes), 2, P], F32, tag="work", name="turned")
            for n, g in enumerate(passes):
                for u in (0, 1):
                    first = 2 * P * g + u
                    nc.tensor.transpose(
                        turned[:, n, u, :], words[:, first : 2 * P * (g + 1) : 2], ident[:]
                    )
            return turned

        def copy_out(turned, passes=range(PASSES)):
            grouped = stage.tile([P, len(passes) * 4 * P], BF16, align_bytes=64, tag="grouped", name="grouped")
            nc.scalar.copy(
                out=grouped[:].bitcast(F32).rearrange("q (g r u) -> q g r u", g=len(passes), u=2),
                in_=turned[:].rearrange("q g u r -> q g r u"),
            )
            return grouped

        def quantise(i, grouped, passes=range(PASSES)):
            window = slice(passes[0], passes[-1] + 1)
            nc.vector.quantize_mx(
                out=codes[:, i, window].rearrange("q g r -> q (g r)").bitcast(FP8X4),
                scales=scales[:, i, window].rearrange("q g r -> q (g r)"),
                in_=grouped[:],
            )

        def project(acc_columns, i):
            for b in X_TILES:
                for g in range(PASSES):
                    nc.tensor.matmul_mx(
                        out=acc_columns[:, b, :],
                        lhsT=codes[:, b, g, :].bitcast(FP8X4),
                        lhsT_scale=scales[:, b, g, :],
                        rhs=codes[:, i, g, :].bitcast(FP8X4),
                        rhs_scale=scales[:, i, g, :],
                        start=(g == 0),
                        stop=(g == PASSES - 1),
                    )

        def project_pair(tiles):
            acc = psum_acc.tile([P, B, 2, HALF], F32, tag="acc", name="acc")
            for half, i in enumerate(tiles):
                project(acc[:, :, half, :], i)
            return acc

        bias_rot = consts.tile([P, 2, 2, HALF], F32)

        def rotate_cos(w, acc):
            rotated = results.tile([P, B, 2, HALF], F32, name="rotated%d" % w)
            nc.vector.scalar_tensor_tensor(
                out=rotated[:].rearrange("p b h j -> p b (h j)"),
                in0=acc[:].rearrange("p b h j -> p b (h j)"),
                scalar=cos,
                in1=bias_rot[:, w].rearrange("p h j -> p (h j)").unsqueeze(1).to_broadcast([P, B, E]),
                op0=ALU.mult, op1=ALU.add,
            )
            return rotated

        def rotate_sin(acc, rotated, half):
            nc.vector.scalar_tensor_tensor(
                out=rotated[:, :, half, :], in0=acc[:, :, 1 - half, :],
                scalar=(neg_sin, sin)[half], in1=rotated[:, :, half, :],
                op0=ALU.mult, op1=ALU.add,
            )

        def store(rotated, out_w):
            nc.sync.dma_start(
                out=out_w.rearrange("b s e -> s b e"),
                in_=rotated[:].rearrange("p b h j -> p b (h j)"),
            )

        def add_store_v(half, acc_v):
            columns = slice(half * HALF, (half + 1) * HALF)
            v_half = results.tile([P, B, HALF], F32, name="v_half%d" % half)
            nc.vector.tensor_tensor(
                out=v_half[:], in0=acc_v[:],
                in1=bias_v[:, columns].unsqueeze(1).to_broadcast([P, B, HALF]), op=ALU.add,
            )
            nc.sync.dma_start(out=out_2.rearrange("b s e -> s b e")[:, :, columns], in_=v_half[:])

        bias_kq_bank = psum_acc.tile([P, 2 * E], F32, tag="acc", name="bias_kq_bank")
        bias_v_bank = psum_work.tile([P, E], F32, tag="work", name="bias_v_bank")
        bias_kq = bias_kq_bank[:].rearrange("p (w j e) -> p w j e", w=2, e=2)
        bias_v = consts.tile([P, E], F32)

        def spread_biases():
            nc.tensor.matmul(
                out=bias_kq_bank[:], lhsT=ones[:], rhs=bias_rows[:, 0 : 2 * E], start=True, stop=True
            )
            nc.tensor.matmul(
                out=bias_v_bank[:], lhsT=ones[:], rhs=bias_rows[:, 2 * E : 3 * E],
                start=True, stop=True,
            )

        def rotate_bias_sin(half):
            nc.vector.tensor_scalar(
                out=bias_rot[:, :, half, :], in0=bias_kq[:, :, :, 1 - half],
                scalar1=(neg_sin, sin)[half], scalar2=None, op0=ALU.mult,
            )

        def rotate_bias_cos(half):
            nc.vector.scalar_tensor_tensor(
                out=bias_rot[:, :, half, :], in0=bias_kq[:, :, :, half], scalar=cos,
                in1=bias_rot[:, :, half, :], op0=ALU.mult, op1=ALU.add,
            )

        with tc.manual_schedule():
            g_parts = [range(g, g + 1) for g in range(PASSES)]
            turned_x0 = [transpose(0, part) for part in g_parts]
            grouped_x0 = [copy_out(t, part) for t, part in zip(turned_x0, g_parts)]
            turned = transpose(1)
            for part, grouped_half in zip(g_parts, grouped_x0):
                quantise(0, grouped_half, part)
            grouped = copy_out(turned)
            turned = transpose(2)
            quantise(1, grouped)
            grouped = copy_out(turned)
            spread_biases()
            turned = transpose(3)
            nc.scalar.copy(out=bias_v[:], in_=bias_v_bank[:])
            rotate_bias_sin(0)
            quantise(2, grouped)
            rotate_bias_sin(1)
            grouped = copy_out(turned)
            turned = transpose(4)
            quantise(3, grouped)
            rotate_bias_cos(0)
            grouped = copy_out(turned)
            turned = transpose(5)
            quantise(4, grouped)
            rotate_bias_cos(1)
            grouped = copy_out(turned)
            acc_k = project_pair(K_TILES)
            turned = transpose(6)
            quantise(5, grouped)
            rotated_k = rotate_cos(0, acc_k)
            grouped = copy_out(turned)
            acc_q = project_pair(Q_TILES)
            turned_v1 = [transpose(7, part) for part in g_parts]
            rotate_sin(acc_k, rotated_k, 0)
            rotate_sin(acc_k, rotated_k, 1)
            store(rotated_k, out_0)
            quantise(6, grouped)
            grouped_v1 = [copy_out(t, part) for t, part in zip(turned_v1, g_parts)]
            acc_v0 = psum_acc.tile([P, B, HALF], F32, tag="acc", name="acc_v0")
            project(acc_v0, 6)
            rotated_q = rotate_cos(1, acc_q)
            quantise(7, grouped_v1[0], g_parts[0])
            quantise(7, grouped_v1[1], g_parts[1])
            acc_v1 = psum_acc.tile([P, B, HALF], F32, tag="acc", name="acc_v1")
            project(acc_v1, 7)
            rotate_sin(acc_q, rotated_q, 0)
            rotate_sin(acc_q, rotated_q, 1)
            store(rotated_q, out_1)
            add_store_v(0, acc_v0)
            add_store_v(1, acc_v1)
